import numpy as np
import ml_dtypes


def mxq(x, axis, fmt="e4m3"):
    dtype, down = {"e4m3": (ml_dtypes.float8_e4m3fn, 7), "e5m2": (ml_dtypes.float8_e5m2, 14)}[fmt]
    v = np.moveaxis(np.asarray(x, np.float32).astype(ml_dtypes.bfloat16).astype(np.float64), axis, -1)
    blocks = v.reshape(v.shape[:-1] + (-1, 32))
    amax = np.abs(blocks).max(-1, keepdims=True)
    byte = np.maximum(np.where(amax > 0, np.frexp(amax)[1] - 1 + 127, 0) - down, 1)
    scale = np.exp2(byte - 127.0)
    codes = (blocks / scale).astype(np.float32).astype(dtype).astype(np.float64)
    return np.moveaxis((codes * scale).reshape(v.shape), -1, axis)


WIDE = False


def mx_kscale(k):
    if not WIDE:
        return np.ones(k)
    levels = np.array([20, -20, 10, -10, 0])
    a = np.random.permutation(np.resize(levels, k // 512 * 4)).reshape(k // 512, 4)
    idx = np.arange(k)
    return np.exp2(a[idx // 512, idx % 128 // 32])


BF16 = ml_dtypes.bfloat16


def bf(x):
    return np.asarray(x, np.float32).astype(BF16)


def f64(x):
    return np.asarray(x).astype(np.float64)


N, E, C, D1, D2 = 1024, 2048, 512, 2, 2
T1 = D1 + 1


def shift_down(y, k):
    return np.pad(y, ((k, 0), (0, 0)))[:y.shape[0]] if k > 0 else y


def shift_up(d, k):
    return np.pad(d[k:], ((0, k), (0, 0))) if k > 0 else d


def window_tanh(x, W1, b1):
    S = sum(shift_down(x @ W1[k], k) for k in range(T1))
    cnt1 = np.minimum(np.arange(N), D1) + 1.0
    return np.tanh(S + cnt1[:, None] * b1[0])


def setup_inputs():
    s = np.asarray(mx_kscale(N), np.float64)
    sm = np.maximum(s, np.maximum(np.concatenate([s[:1], s[:-1]]), np.concatenate([s[:2], s[:-2]])))
    x0 = bf(np.random.standard_normal((N, E)))
    W1 = bf(np.random.standard_normal((T1, E, C)) * 0.4 / np.sqrt(E))
    b1 = bf(np.random.standard_normal((1, C)) * 0.25)
    g = bf(np.random.standard_normal((N, C)) * np.exp2(np.random.randint(-12, 1, (N, 1))) / sm[:, None])
    y = window_tanh(f64(x0), f64(W1), f64(b1))
    return {"x": bf(f64(x0) * s[:, None]), "W1": W1, "b1": b1, "y": np.asarray(y, np.float32), "grad_out": g}


def reference(x, W1, b1, y, grad_out):
    yf = f64(y)
    dz = f64(grad_out) * (1.0 - yf * yf)
    xq = mxq(f64(x), 0, "e4m3")
    return np.stack([(xq.T @ mxq(shift_up(dz, k), 0, "e5m2")) for k in range(T1)])

@@ -1,0 +1,170 @@
+from contextlib import ExitStack
+
+import concourse.mybir as mybir
+from concourse.masks import make_identity
+
+F32 = mybir.dt.float32
+BF16 = mybir.dt.bfloat16
+U32 = mybir.dt.uint32
+U8 = mybir.dt.uint8
+E4M3_X4 = mybir.dt.float8_e4m3fn_x4
+E5M2_X4 = mybir.dt.float8_e5m2_x4
+ALU = mybir.AluOpType
+ACT = mybir.ActivationFunctionType
+
+TOKENS = 1024
+E = 2048
+C = 512
+TAPS = 3
+
+P = 128
+PACK = 4
+PASSES = TOKENS // (P * PACK)
+HALO = TAPS - 1
+QUAD = 4
+QUAD_COLS = QUAD * P
+QUADS = E // QUAD_COLS
+HALVES = 2
+QUADS_PER_HALF = QUADS // HALVES
+RUN = 4
+
+FLOPS = 2 * TOKENS * E * C * TAPS
+BYTES = 2 * TOKENS * E + 4 * TOKENS * C + 2 * TOKENS * C + 4 * TAPS * E * C
+
+
+def tile_predictor_pa_v_kernel(tc, x, W1, b1, y, grad_out, out):
+    nc = tc.nc
+    with ExitStack() as ctx:
+        keep = ctx.enter_context(tc.tile_pool(name="keep", bufs=1))
+        groups = ctx.enter_context(tc.tile_pool(name="groups", bufs=2))
+        stages = ctx.enter_context(tc.tile_pool(name="stages", bufs=4))
+        banks = ctx.enter_context(tc.psum_pool(name="banks", bufs=8))
+
+        identity = keep.tile([P, P], BF16)
+        make_identity(nc, identity[:])
+        from_next = keep.tile([P, P], BF16)
+        nc.vector.memset(from_next[:], 0.0)
+        nc.vector.tensor_copy(out=from_next[:, 0 : P - 1], in_=identity[:, 1:P])
+        from_first = keep.tile([P, P], BF16)
+        nc.vector.memset(from_first[:], 0.0)
+        nc.vector.tensor_copy(out=from_first[:, P - 1 : P], in_=identity[:, 0:1])
+
+        y_rows = y.rearrange("(c p j) w -> c p j w", c=PASSES, j=PACK)
+        g_rows = grad_out.rearrange("(c p j) w -> c p j w", c=PASSES, j=PACK)
+        x_rows = x.rearrange("(c p j) e -> c p j e", c=PASSES, j=PACK)
+        y_sb = keep.tile([P, PASSES, PACK, C], F32)
+        g_sb = keep.tile([P, PASSES, PACK, C], BF16)
+        x_sb = keep.tile([P, QUADS, PASSES, PACK, QUAD_COLS], BF16)
+        for c in range(PASSES):
+            nc.sync.dma_start(out=g_sb[:, c], in_=g_rows[c])
+            nc.sync.dma_start(out=y_sb[:, c, 0:HALO, :], in_=y_rows[c, :, 0:HALO, :])
+            nc.sync.dma_start(out=y_sb[:, c, HALO:PACK, :], in_=y_rows[c, :, HALO:PACK, :])
+        for q in range(QUADS):
+            for c in range(PASSES):
+                nc.sync.dma_start(
+                    out=x_sb[:, q, c], in_=x_rows[c, :, :, q * QUAD_COLS : (q + 1) * QUAD_COLS]
+                )
+
+        d_grouped = keep.tile([P, TAPS, PASSES, C, PACK], BF16, align_bytes=64)
+        d_codes = keep.tile([P, TAPS, PASSES, C], U32, align_bytes=64)
+        d_scales = keep.tile([P, TAPS, PASSES, C], U8, align_bytes=64)
+        x_codes = keep.tile([P, QUADS, PASSES, QUAD, P], U32, align_bytes=64)
+        x_scales = keep.tile([P, QUADS, PASSES, QUAD, P], U8, align_bytes=64)
+
+        def copy_of_pass(c, scalar_helps):
+            return nc.scalar.copy if scalar_helps and c == 0 else nc.vector.tensor_copy
+
+        def regroup_d(k, c, copy):
+            copy(
+                out=d_grouped[:, k, c].rearrange("p (b i) t -> p b t i", i=RUN),
+                in_=dz[:, c, k : k + PACK, :].rearrange("p t (b i) -> p b t i", i=RUN),
+            )
+
+        def quantise_d(k):
+            nc.vector.quantize_mx(
+                out=d_codes[:, k].rearrange("p c w -> p (c w)").bitcast(E5M2_X4),
+                scales=d_scales[:, k].rearrange("p c w -> p (c w)"),
+                in_=d_grouped[:, k].rearrange("p c w t -> p (c w t)"),
+            )
+
+        def prepare_d(k, scalar_helps):
+            for c in range(PASSES):
+                regroup_d(k, c, copy_of_pass(c, scalar_helps))
+            quantise_d(k)
+
+        def prepare_x(q, scalar_helps):
+            x_grouped = groups.tile([P, PASSES, QUAD, P, PACK], BF16, align_bytes=64)
+            for c in range(PASSES):
+                copy_of_pass(c, scalar_helps)(
+                    out=x_grouped[:, c].rearrange("p i m t -> p m t i"),
+                    in_=x_sb[:, q, c].rearrange("p t (m i) -> p m t i", i=QUAD),
+                )
+            nc.vector.quantize_mx(
+                out=x_codes[:, q].rearrange("p c i m -> p (c i m)").bitcast(E4M3_X4),
+                scales=x_scales[:, q].rearrange("p c i m -> p (c i m)"),
+                in_=x_grouped[:].rearrange("p c i m t -> p (c i m t)"),
+            )
+
+        def multiply(q, k, vector_helps):
+            stage = stages.tile([P, QUAD, C], F32)
+            for i in range(QUAD):
+                product = banks.tile([P, C], F32, tag="bank")
+                for c in range(PASSES):
+                    nc.tensor.matmul_mx(
+                        out=product[:],
+                        lhsT=x_codes[:, q, c, i, :].bitcast(E4M3_X4),
+                        lhsT_scale=x_scales[:, q, c, i, :],
+                        rhs=d_codes[:, k, c, :].bitcast(E5M2_X4),
+                        rhs_scale=d_scales[:, k, c, :],
+                        start=(c == 0),
+                        stop=(c == PASSES - 1),
+                    )
+                if vector_helps and i % 2 == 1:
+                    nc.vector.tensor_copy(out=stage[:, i, :], in_=product[:])
+                else:
+                    nc.scalar.copy(out=stage[:, i, :], in_=product[:])
+            nc.sync.dma_start(
+                out=out[k, q * QUAD_COLS : (q + 1) * QUAD_COLS, :].rearrange("(m i) n -> m i n", i=QUAD),
+                in_=stage[:],
+            )
+
+        minus_g = keep.tile([P, PASSES, PACK, C], BF16)
+        y_squared = keep.tile([P, PASSES, PACK, C], F32)
+        dz = keep.tile([P, PASSES, PACK + HALO, C], BF16)
+        for c in range(PASSES):
+            nc.vector.tensor_scalar_mul(out=minus_g[:, c], in0=g_sb[:, c], scalar1=-1.0)
+            for first in range(0, PACK, HALO):
+                rows = slice(first, first + HALO)
+                nc.scalar.activation(out=y_squared[:, c, rows, :], in_=y_sb[:, c, rows, :], func=ACT.Square)
+                nc.vector.scalar_tensor_tensor(
+                    out=dz[:, c, rows, :],
+                    in0=y_squared[:, c, rows, :],
+                    scalar=1.0,
+                    in1=minus_g[:, c, rows, :],
+                    op0=ALU.subtract,
+                    op1=ALU.mult,
+                )
+            regroup_d(0, c, nc.vector.tensor_copy)
+        quantise_d(0)
+        prepare_x(0, scalar_helps=True)
+
+        for c in range(PASSES):
+            for r in range(HALO):
+                moved = banks.tile([P, C], F32, tag="bank")
+                last_pass = c == PASSES - 1
+                nc.tensor.matmul(out=moved[:], lhsT=from_next[:], rhs=dz[:, c, r, :], start=True, stop=last_pass)
+                if not last_pass:
+                    nc.tensor.matmul(
+                        out=moved[:], lhsT=from_first[:], rhs=dz[:, c + 1, r, :], start=False, stop=True
+                    )
+                nc.scalar.copy(out=dz[:, c, PACK + r, :], in_=moved[:])
+        prepare_x(1, scalar_helps=True)
+
+        for half in range(HALVES):
+            for k in range(TAPS):
+                if half == 0 and k + 1 < TAPS:
+                    prepare_d(k + 1, scalar_helps=(k == 0))
+                if half + 1 < HALVES and k >= 1:
+                    prepare_x((half + 1) * QUADS_PER_HALF + k - 1, scalar_helps=False)
+                for q in range(half * QUADS_PER_HALF, (half + 1) * QUADS_PER_HALF):
+                    multiply(q, k, vector_helps=(half == HALVES - 1))

@@ -56,8 +56,8 @@ def tile_predictor_pa_v_kernel(tc, x, W1, b1, y, grad_out, out):
         g_sb = keep.tile([P, PASSES, PACK, C], BF16)
         x_sb = keep.tile([P, QUADS, PASSES, PACK, QUAD_COLS], BF16)
         for c in range(PASSES):
-            nc.sync.dma_start(out=g_sb[:, c], in_=g_rows[c])
             nc.sync.dma_start(out=y_sb[:, c, 0:HALO, :], in_=y_rows[c, :, 0:HALO, :])
+            nc.sync.dma_start(out=g_sb[:, c], in_=g_rows[c])
             nc.sync.dma_start(out=y_sb[:, c, HALO:PACK, :], in_=y_rows[c, :, HALO:PACK, :])
         for q in range(QUADS):
             for c in range(PASSES):
@@ -71,39 +71,40 @@ def tile_predictor_pa_v_kernel(tc, x, W1, b1, y, grad_out, out):
         x_codes = keep.tile([P, QUADS, PASSES, QUAD, P], U32, align_bytes=64)
         x_scales = keep.tile([P, QUADS, PASSES, QUAD, P], U8, align_bytes=64)
 
-        def copy_of_pass(c, scalar_helps):
-            return nc.scalar.copy if scalar_helps and c == 0 else nc.vector.tensor_copy
-
-        def regroup_d(k, c, copy):
-            copy(
+        def regroup_d(k, c):
+            nc.vector.tensor_scalar_mul(
                 out=d_grouped[:, k, c].rearrange("p (b i) t -> p b t i", i=RUN),
-                in_=dz[:, c, k : k + PACK, :].rearrange("p t (b i) -> p b t i", i=RUN),
+                in0=minus_dz[:, c, k : k + PACK, :].rearrange("p t (b i) -> p b t i", i=RUN),
+                scalar1=-1.0,
             )
 
         def quantise_d(k):
-            nc.vector.quantize_mx(
-                out=d_codes[:, k].rearrange("p c w -> p (c w)").bitcast(E5M2_X4),
-                scales=d_scales[:, k].rearrange("p c w -> p (c w)"),
-                in_=d_grouped[:, k].rearrange("p c w t -> p (c w t)"),
-            )
-
-        def prepare_d(k, scalar_helps):
             for c in range(PASSES):
-                regroup_d(k, c, copy_of_pass(c, scalar_helps))
+                nc.vector.quantize_mx(
+                    out=d_codes[:, k, c, :].bitcast(E5M2_X4),
+                    scales=d_scales[:, k, c, :],
+                    in_=d_grouped[:, k, c].rearrange("p w t -> p (w t)"),
+                )
+
+        def prepare_d(k):
+            for c in range(PASSES):
+                regroup_d(k, c)
             quantise_d(k)
 
         def prepare_x(q, scalar_helps):
             x_grouped = groups.tile([P, PASSES, QUAD, P, PACK], BF16, align_bytes=64)
             for c in range(PASSES):
-                copy_of_pass(c, scalar_helps)(
+                copy = nc.scalar.copy if scalar_helps and c == 0 else nc.vector.tensor_copy
+                copy(
                     out=x_grouped[:, c].rearrange("p i m t -> p m t i"),
                     in_=x_sb[:, q, c].rearrange("p t (m i) -> p m t i", i=QUAD),
                 )
-            nc.vector.quantize_mx(
-                out=x_codes[:, q].rearrange("p c i m -> p (c i m)").bitcast(E4M3_X4),
-                scales=x_scales[:, q].rearrange("p c i m -> p (c i m)"),
-                in_=x_grouped[:].rearrange("p c i m t -> p (c i m t)"),
-            )
+            for c in range(PASSES):
+                nc.vector.quantize_mx(
+                    out=x_codes[:, q, c].rearrange("p i m -> p (i m)").bitcast(E4M3_X4),
+                    scales=x_scales[:, q, c].rearrange("p i m -> p (i m)"),
+                    in_=x_grouped[:, c].rearrange("p i m t -> p (i m t)"),
+                )
 
         def multiply(q, k, vector_helps):
             stage = stages.tile([P, QUAD, C], F32)
@@ -128,23 +129,21 @@ def tile_predictor_pa_v_kernel(tc, x, W1, b1, y, grad_out, out):
                 in_=stage[:],
             )
 
-        minus_g = keep.tile([P, PASSES, PACK, C], BF16)
         y_squared = keep.tile([P, PASSES, PACK, C], F32)
-        dz = keep.tile([P, PASSES, PACK + HALO, C], BF16)
+        minus_dz = keep.tile([P, PASSES, PACK + HALO, C], BF16)
         for c in range(PASSES):
-            nc.vector.tensor_scalar_mul(out=minus_g[:, c], in0=g_sb[:, c], scalar1=-1.0)
             for first in range(0, PACK, HALO):
                 rows = slice(first, first + HALO)
                 nc.scalar.activation(out=y_squared[:, c, rows, :], in_=y_sb[:, c, rows, :], func=ACT.Square)
                 nc.vector.scalar_tensor_tensor(
-                    out=dz[:, c, rows, :],
+                    out=minus_dz[:, c, rows, :],
                     in0=y_squared[:, c, rows, :],
                     scalar=1.0,
-                    in1=minus_g[:, c, rows, :],
+                    in1=g_sb[:, c, rows, :],
                     op0=ALU.subtract,
                     op1=ALU.mult,
                 )
-            regroup_d(0, c, nc.vector.tensor_copy)
+            regroup_d(0, c)
         quantise_d(0)
         prepare_x(0, scalar_helps=True)
 
@@ -152,18 +151,18 @@ def tile_predictor_pa_v_kernel(tc, x, W1, b1, y, grad_out, out):
             for r in range(HALO):
                 moved = banks.tile([P, C], F32, tag="bank")
                 last_pass = c == PASSES - 1
-                nc.tensor.matmul(out=moved[:], lhsT=from_next[:], rhs=dz[:, c, r, :], start=True, stop=last_pass)
+                nc.tensor.matmul(out=moved[:], lhsT=from_next[:], rhs=minus_dz[:, c, r, :], start=True, stop=last_pass)
                 if not last_pass:
                     nc.tensor.matmul(
-                        out=moved[:], lhsT=from_first[:], rhs=dz[:, c + 1, r, :], start=False, stop=True
+                        out=moved[:], lhsT=from_first[:], rhs=minus_dz[:, c + 1, r, :], start=False, stop=True
                     )
-                nc.scalar.copy(out=dz[:, c, PACK + r, :], in_=moved[:])
+                nc.scalar.copy(out=minus_dz[:, c, PACK + r, :], in_=moved[:])
         prepare_x(1, scalar_helps=True)
 
         for half in range(HALVES):
             for k in range(TAPS):
                 if half == 0 and k + 1 < TAPS:
-                    prepare_d(k + 1, scalar_helps=(k == 0))
+                    prepare_d(k + 1)
                 if half + 1 < HALVES and k >= 1:
                     prepare_x((half + 1) * QUADS_PER_HALF + k - 1, scalar_helps=False)
                 for q in range(half * QUADS_PER_HALF, (half + 1) * QUADS_PER_HALF):

@@ -27,6 +27,7 @@ QUADS = E // QUAD_COLS
 HALVES = 2
 QUADS_PER_HALF = QUADS // HALVES
 RUN = 4
+STORE_TILES = 2
 
 FLOPS = 2 * TOKENS * E * C * TAPS
 BYTES = 2 * TOKENS * E + 4 * TOKENS * C + 2 * TOKENS * C + 4 * TAPS * E * C
@@ -71,12 +72,13 @@ def tile_predictor_pa_v_kernel(tc, x, W1, b1, y, grad_out, out):
         x_codes = keep.tile([P, QUADS, PASSES, QUAD, P], U32, align_bytes=64)
         x_scales = keep.tile([P, QUADS, PASSES, QUAD, P], U8, align_bytes=64)
 
-        def regroup_d(k, c):
-            nc.vector.tensor_scalar_mul(
-                out=d_grouped[:, k, c].rearrange("p (b i) t -> p b t i", i=RUN),
-                in0=minus_dz[:, c, k : k + PACK, :].rearrange("p t (b i) -> p b t i", i=RUN),
-                scalar1=-1.0,
-            )
+        def regroup_d(k, c, scalar_helps):
+            grouped = d_grouped[:, k, c].rearrange("p (b i) t -> p b t i", i=RUN)
+            rows = minus_dz[:, c, k : k + PACK, :].rearrange("p t (b i) -> p b t i", i=RUN)
+            if scalar_helps and c == 0:
+                nc.scalar.mul(out=grouped, in_=rows, mul=-1.0)
+            else:
+                nc.vector.tensor_scalar_mul(out=grouped, in0=rows, scalar1=-1.0)
 
         def quantise_d(k):
             for c in range(PASSES):
@@ -86,9 +88,9 @@ def tile_predictor_pa_v_kernel(tc, x, W1, b1, y, grad_out, out):
                     in_=d_grouped[:, k, c].rearrange("p w t -> p (w t)"),
                 )
 
-        def prepare_d(k):
+        def prepare_d(k, scalar_helps):
             for c in range(PASSES):
-                regroup_d(k, c)
+                regroup_d(k, c, scalar_helps)
             quantise_d(k)
 
         def prepare_x(q, scalar_helps):
@@ -108,6 +110,7 @@ def tile_predictor_pa_v_kernel(tc, x, W1, b1, y, grad_out, out):
 
         def multiply(q, k, vector_helps):
             stage = stages.tile([P, QUAD, C], F32)
+            out_rows = out[k, q * QUAD_COLS : (q + 1) * QUAD_COLS, :].rearrange("(m i) n -> m i n", i=QUAD)
             for i in range(QUAD):
                 product = banks.tile([P, C], F32, tag="bank")
                 for c in range(PASSES):
@@ -124,10 +127,9 @@ def tile_predictor_pa_v_kernel(tc, x, W1, b1, y, grad_out, out):
                     nc.vector.tensor_copy(out=stage[:, i, :], in_=product[:])
                 else:
                     nc.scalar.copy(out=stage[:, i, :], in_=product[:])
-            nc.sync.dma_start(
-                out=out[k, q * QUAD_COLS : (q + 1) * QUAD_COLS, :].rearrange("(m i) n -> m i n", i=QUAD),
-                in_=stage[:],
-            )
+                if (i + 1) % STORE_TILES == 0:
+                    tiles = slice(i + 1 - STORE_TILES, i + 1)
+                    nc.sync.dma_start(out=out_rows[:, tiles, :], in_=stage[:, tiles, :])
 
         y_squared = keep.tile([P, PASSES, PACK, C], F32)
         minus_dz = keep.tile([P, PASSES, PACK + HALO, C], BF16)
@@ -143,26 +145,28 @@ def tile_predictor_pa_v_kernel(tc, x, W1, b1, y, grad_out, out):
                     op0=ALU.subtract,
                     op1=ALU.mult,
                 )
-            regroup_d(0, c)
+            regroup_d(0, c, scalar_helps=False)
         quantise_d(0)
         prepare_x(0, scalar_helps=True)
 
         for c in range(PASSES):
+            moved = banks.tile([P, HALO, C], BF16, tag="bank")
+            last_pass = c == PASSES - 1
             for r in range(HALO):
-                moved = banks.tile([P, C], F32, tag="bank")
-                last_pass = c == PASSES - 1
-                nc.tensor.matmul(out=moved[:], lhsT=from_next[:], rhs=minus_dz[:, c, r, :], start=True, stop=last_pass)
+                nc.tensor.matmul(
+                    out=moved[:, r, :], lhsT=from_next[:], rhs=minus_dz[:, c, r, :], start=True, stop=last_pass
+                )
                 if not last_pass:
                     nc.tensor.matmul(
-                        out=moved[:], lhsT=from_first[:], rhs=minus_dz[:, c + 1, r, :], start=False, stop=True
+                        out=moved[:, r, :], lhsT=from_first[:], rhs=minus_dz[:, c + 1, r, :], start=False, stop=True
                     )
-                nc.scalar.copy(out=minus_dz[:, c, PACK + r, :], in_=moved[:])
+            nc.scalar.copy(out=minus_dz[:, c, PACK : PACK + HALO, :], in_=moved[:])
         prepare_x(1, scalar_helps=True)
 
         for half in range(HALVES):
             for k in range(TAPS):
                 if half == 0 and k + 1 < TAPS:
-                    prepare_d(k + 1)
+                    prepare_d(k + 1, scalar_helps=(k == 0))
                 if half + 1 < HALVES and k >= 1:
                     prepare_x((half + 1) * QUADS_PER_HALF + k - 1, scalar_helps=False)
                 for q in range(half * QUADS_PER_HALF, (half + 1) * QUADS_PER_HALF):

from contextlib import ExitStack

import concourse.mybir as mybir
from concourse.masks import make_identity

F32 = mybir.dt.float32
BF16 = mybir.dt.bfloat16
U32 = mybir.dt.uint32
U8 = mybir.dt.uint8
E4M3_X4 = mybir.dt.float8_e4m3fn_x4
E5M2_X4 = mybir.dt.float8_e5m2_x4
ALU = mybir.AluOpType
ACT = mybir.ActivationFunctionType

TOKENS = 1024
E = 2048
C = 512
TAPS = 3

P = 128
PACK = 4
PASSES = TOKENS // (P * PACK)
HALO = TAPS - 1
QUAD = 4
QUAD_COLS = QUAD * P
QUADS = E // QUAD_COLS
HALVES = 2
QUADS_PER_HALF = QUADS // HALVES
RUN = 4
STORE_TILES = 2

FLOPS = 2 * TOKENS * E * C * TAPS
BYTES = 2 * TOKENS * E + 4 * TOKENS * C + 2 * TOKENS * C + 4 * TAPS * E * C


def tile_predictor_pa_v_kernel(tc, x, W1, b1, y, grad_out, out):
    nc = tc.nc
    with ExitStack() as ctx:
        keep = ctx.enter_context(tc.tile_pool(name="keep", bufs=1))
        groups = ctx.enter_context(tc.tile_pool(name="groups", bufs=2))
        stages = ctx.enter_context(tc.tile_pool(name="stages", bufs=4))
        banks = ctx.enter_context(tc.psum_pool(name="banks", bufs=8))

        identity = keep.tile([P, P], BF16)
        make_identity(nc, identity[:])
        from_next = keep.tile([P, P], BF16)
        nc.vector.memset(from_next[:], 0.0)
        nc.vector.tensor_copy(out=from_next[:, 0 : P - 1], in_=identity[:, 1:P])
        from_first = keep.tile([P, P], BF16)
        nc.vector.memset(from_first[:], 0.0)
        nc.vector.tensor_copy(out=from_first[:, P - 1 : P], in_=identity[:, 0:1])

        y_rows = y.rearrange("(c p j) w -> c p j w", c=PASSES, j=PACK)
        g_rows = grad_out.rearrange("(c p j) w -> c p j w", c=PASSES, j=PACK)
        x_rows = x.rearrange("(c p j) e -> c p j e", c=PASSES, j=PACK)
        y_sb = keep.tile([P, PASSES, PACK, C], F32)
        g_sb = keep.tile([P, PASSES, PACK, C], BF16)
        x_sb = keep.tile([P, QUADS, PASSES, PACK, QUAD_COLS], BF16)
        for c in range(PASSES):
            nc.sync.dma_start(out=y_sb[:, c, 0:HALO, :], in_=y_rows[c, :, 0:HALO, :])
            nc.sync.dma_start(out=g_sb[:, c], in_=g_rows[c])
            nc.sync.dma_start(out=y_sb[:, c, HALO:PACK, :], in_=y_rows[c, :, HALO:PACK, :])
        for q in range(QUADS):
            for c in range(PASSES):
                nc.sync.dma_start(
                    out=x_sb[:, q, c], in_=x_rows[c, :, :, q * QUAD_COLS : (q + 1) * QUAD_COLS]
                )

        d_grouped = keep.tile([P, TAPS, PASSES, C, PACK], BF16, align_bytes=64)
        d_codes = keep.tile([P, TAPS, PASSES, C], U32, align_bytes=64)
        d_scales = keep.tile([P, TAPS, PASSES, C], U8, align_bytes=64)
        x_codes = keep.tile([P, QUADS, PASSES, QUAD, P], U32, align_bytes=64)
        x_scales = keep.tile([P, QUADS, PASSES, QUAD, P], U8, align_bytes=64)

        def regroup_d(k, c, scalar_helps):
            grouped = d_grouped[:, k, c].rearrange("p (b i) t -> p b t i", i=RUN)
            rows = minus_dz[:, c, k : k + PACK, :].rearrange("p t (b i) -> p b t i", i=RUN)
            if scalar_helps and c == 0:
                nc.scalar.mul(out=grouped, in_=rows, mul=-1.0)
            else:
                nc.vector.tensor_scalar_mul(out=grouped, in0=rows, scalar1=-1.0)

        def quantise_d(k):
            for c in range(PASSES):
                nc.vector.quantize_mx(
                    out=d_codes[:, k, c, :].bitcast(E5M2_X4),
                    scales=d_scales[:, k, c, :],
                    in_=d_grouped[:, k, c].rearrange("p w t -> p (w t)"),
                )

        def prepare_d(k, scalar_helps):
            for c in range(PASSES):
                regroup_d(k, c, scalar_helps)
            quantise_d(k)

        def prepare_x(q, scalar_helps):
            x_grouped = groups.tile([P, PASSES, QUAD, P, PACK], BF16, align_bytes=64)
            for c in range(PASSES):
                copy = nc.scalar.copy if scalar_helps and c == 0 else nc.vector.tensor_copy
                copy(
                    out=x_grouped[:, c].rearrange("p i m t -> p m t i"),
                    in_=x_sb[:, q, c].rearrange("p t (m i) -> p m t i", i=QUAD),
                )
            for c in range(PASSES):
                nc.vector.quantize_mx(
                    out=x_codes[:, q, c].rearrange("p i m -> p (i m)").bitcast(E4M3_X4),
                    scales=x_scales[:, q, c].rearrange("p i m -> p (i m)"),
                    in_=x_grouped[:, c].rearrange("p i m t -> p (i m t)"),
                )

        def multiply(q, k, vector_helps):
            stage = stages.tile([P, QUAD, C], F32)
            out_rows = out[k, q * QUAD_COLS : (q + 1) * QUAD_COLS, :].rearrange("(m i) n -> m i n", i=QUAD)
            for i in range(QUAD):
                product = banks.tile([P, C], F32, tag="bank")
                for c in range(PASSES):
                    nc.tensor.matmul_mx(
                        out=product[:],
                        lhsT=x_codes[:, q, c, i, :].bitcast(E4M3_X4),
                        lhsT_scale=x_scales[:, q, c, i, :],
                        rhs=d_codes[:, k, c, :].bitcast(E5M2_X4),
                        rhs_scale=d_scales[:, k, c, :],
                        start=(c == 0),
                        stop=(c == PASSES - 1),
                    )
                if vector_helps and i % 2 == 1:
                    nc.vector.tensor_copy(out=stage[:, i, :], in_=product[:])
                else:
                    nc.scalar.copy(out=stage[:, i, :], in_=product[:])
                if (i + 1) % STORE_TILES == 0:
                    tiles = slice(i + 1 - STORE_TILES, i + 1)
                    nc.sync.dma_start(out=out_rows[:, tiles, :], in_=stage[:, tiles, :])

        y_squared = keep.tile([P, PASSES, PACK, C], F32)
        minus_dz = keep.tile([P, PASSES, PACK + HALO, C], BF16)
        for c in range(PASSES):
            for first in range(0, PACK, HALO):
                rows = slice(first, first + HALO)
                nc.scalar.activation(out=y_squared[:, c, rows, :], in_=y_sb[:, c, rows, :], func=ACT.Square)
                nc.vector.scalar_tensor_tensor(
                    out=minus_dz[:, c, rows, :],
                    in0=y_squared[:, c, rows, :],
                    scalar=1.0,
                    in1=g_sb[:, c, rows, :],
                    op0=ALU.subtract,
                    op1=ALU.mult,
                )
            regroup_d(0, c, scalar_helps=False)
        quantise_d(0)
        prepare_x(0, scalar_helps=True)

        for c in range(PASSES):
            moved = banks.tile([P, HALO, C], BF16, tag="bank")
            last_pass = c == PASSES - 1
            for r in range(HALO):
                nc.tensor.matmul(
                    out=moved[:, r, :], lhsT=from_next[:], rhs=minus_dz[:, c, r, :], start=True, stop=last_pass
                )
                if not last_pass:
                    nc.tensor.matmul(
                        out=moved[:, r, :], lhsT=from_first[:], rhs=minus_dz[:, c + 1, r, :], start=False, stop=True
                    )
            nc.scalar.copy(out=minus_dz[:, c, PACK : PACK + HALO, :], in_=moved[:])
        prepare_x(1, scalar_helps=True)

        for half in range(HALVES):
            for k in range(TAPS):
                if half == 0 and k + 1 < TAPS:
                    prepare_d(k + 1, scalar_helps=(k == 0))
                if half + 1 < HALVES and k >= 1:
                    prepare_x((half + 1) * QUADS_PER_HALF + k - 1, scalar_helps=False)
                for q in range(half * QUADS_PER_HALF, (half + 1) * QUADS_PER_HALF):
                    multiply(q, k, vector_helps=(half == HALVES - 1))
